import numpy as np
import ml_dtypes


def mxq(x, axis, fmt="e4m3"):
    dtype, down = {"e4m3": (ml_dtypes.float8_e4m3fn, 7), "e5m2": (ml_dtypes.float8_e5m2, 14)}[fmt]
    v = np.moveaxis(np.asarray(x, np.float32).astype(ml_dtypes.bfloat16).astype(np.float64), axis, -1)
    blocks = v.reshape(v.shape[:-1] + (-1, 32))
    amax = np.abs(blocks).max(-1, keepdims=True)
    byte = np.maximum(np.where(amax > 0, np.frexp(amax)[1] - 1 + 127, 0) - down, 1)
    scale = np.exp2(byte - 127.0)
    codes = (blocks / scale).astype(np.float32).astype(dtype).astype(np.float64)
    return np.moveaxis((codes * scale).reshape(v.shape), -1, axis)


WIDE = False


def mx_kscale(k):
    if not WIDE:
        return np.ones(k)
    levels = np.array([10, -10, 5, -5, 0])
    if k % 512:
        return np.exp2(np.random.permutation(np.resize(levels, k // 32))).repeat(32)
    a = np.empty((k // 512, 16))
    for p in range(k // 512):
        a[p, :8] = np.random.permutation(np.resize(levels, 8))
        for g in range(8):
            far = levels[np.abs(levels - a[p, g]) >= 10]
            a[p, g + 8] = far[np.random.randint(len(far))]
    return np.exp2(a.ravel()).repeat(32)


BF16 = ml_dtypes.bfloat16


def bf(x):
    return np.asarray(x, np.float32).astype(BF16)


def f64(x):
    return np.asarray(x).astype(np.float64)


S, D, DA, FF = 256, 2048, 2048, 2560
HALF = DA // 2
EPS = 1.1920929e-07
ROPE_BASE = 10000.0


def rms_norm(x, w):
    return x * (1.0 / np.sqrt(np.mean(x * x, axis=-1, keepdims=True) + EPS)) * w


def rope(y, cos, sin):
    y1, y2 = y[:, :HALF], y[:, HALF:]
    return np.concatenate([y1 * cos - y2 * sin, y1 * sin + y2 * cos], axis=-1)


def setup_inputs():
    s = mx_kscale(D)
    angles = np.outer(np.arange(S), 1.0 / ROPE_BASE ** (np.arange(0, DA, 2) / DA))
    return {"x": bf(np.random.standard_normal((S, D))),
            "w_rn1": bf((1.0 + 0.1 * np.random.standard_normal(D)) * s),
            "wq": bf(np.random.standard_normal((DA, D)) / np.sqrt(D) / s[None, :]),
            "wk": bf(np.random.standard_normal((DA, D)) / np.sqrt(D) / s[None, :]),
            "wv": bf(np.random.standard_normal((DA, D)) * 2.0 / np.sqrt(D) / s[None, :]),
            "cos": bf(np.cos(angles)),
            "sin": bf(np.sin(angles))}


def reference(x, w_rn1, wq, wk, wv, cos, sin):
    h = mxq(rms_norm(f64(x), f64(w_rn1)), 1, "e4m3")
    c, sn = f64(cos), f64(sin)
    q = rope(h @ mxq(f64(wq), 1, "e4m3").T, c, sn)
    k = rope(h @ mxq(f64(wk), 1, "e4m3").T, c, sn)
    v = h @ mxq(f64(wv), 1, "e4m3").T
    return q, k, v

@@ -1,0 +1,302 @@
+from contextlib import ExitStack
+
+import concourse.mybir as mybir
+from concourse.masks import make_identity
+
+BF16 = mybir.dt.bfloat16
+F32 = mybir.dt.float32
+U32 = mybir.dt.uint32
+U8 = mybir.dt.uint8
+FP8X4 = mybir.dt.float8_e4m3fn_x4
+ACT = mybir.ActivationFunctionType
+ALU = mybir.AluOpType
+
+P = 128
+S = 256
+D = 2048
+DA = 2048
+HALF = DA // 2
+EPS = 1.1920929e-07
+
+ROW_TILES = S // P
+K_PASS = 4 * P
+PASSES = D // K_PASS
+PASS_WORDS = K_PASS // 2
+ROW_WORDS = D // 2
+BANK = 512
+
+UNIT = 512
+UNITS = 3 * DA // UNIT
+PRODUCTS = UNITS * ROW_TILES
+CHUNK = 256
+CHUNK_TILES = CHUNK // P
+UNIT_CHUNKS = UNIT // CHUNK
+CHUNKS = UNITS * UNIT_CHUNKS
+
+FIRST = 0
+SECOND = 1
+PLAIN = 2
+
+RAW_BUFS = 8
+TABLES_AFTER = 4
+PASS_LAG = 3
+LAST_ROUNDS = 2
+SUM_LAG = 2
+
+FLOPS = 2 * S * D * 3 * DA
+
+
+def tile_llamablock_pa_kernel(tc, x, w_rn1, wq, wk, wv, cos, sin, out_0, out_1, out_2):
+    nc = tc.nc
+
+    def rotary_pair(w, out, col):
+        return [(w, out, col, FIRST), (w, out, HALF + col, SECOND)]
+
+    def plain(block):
+        return [(wv, out_2, block * UNIT, PLAIN)]
+
+    units = (
+        rotary_pair(wq, out_0, 0) + plain(0) + rotary_pair(wq, out_0, UNIT) + plain(1)
+        + rotary_pair(wk, out_1, 0) + rotary_pair(wk, out_1, UNIT) + plain(2) + plain(3)
+    )
+
+    with ExitStack() as ctx:
+        keep = ctx.enter_context(tc.tile_pool(name="keep", bufs=1))
+        raw_pool = ctx.enter_context(tc.tile_pool(name="raw", bufs=RAW_BUFS))
+        grouped_pool = ctx.enter_context(tc.tile_pool(name="grouped", bufs=4))
+        mx_pool = ctx.enter_context(tc.tile_pool(name="mx", bufs=3))
+        first_pool = ctx.enter_context(tc.tile_pool(name="first", bufs=4))
+        second_pool = ctx.enter_context(tc.tile_pool(name="second", bufs=2))
+        plain_pool = ctx.enter_context(tc.tile_pool(name="plain", bufs=3))
+        flip_psum = ctx.enter_context(tc.psum_pool(name="flip", bufs=4))
+        acc_psum = ctx.enter_context(tc.psum_pool(name="acc", bufs=4))
+        ctx.enter_context(tc.manual_schedule())
+
+        raw_of = {}
+        grouped_of = {}
+        codes_of = {}
+        scales_of = {}
+        acc_of = {}
+        rotated = {}
+
+        def load_chunk(c):
+            i, part = divmod(c, UNIT_CHUNKS)
+            w_dram = units[i][0]
+            row = units[i][2] + part * CHUNK
+            raw = raw_pool.tile([P, CHUNK_TILES * D], BF16)
+            nc.sync.dma_start(
+                out=raw[:].rearrange("p (t k) -> p t k", t=CHUNK_TILES),
+                in_=w_dram[row : row + CHUNK, :].rearrange("(t p) k -> p t k", p=P),
+            )
+            raw_of[c] = raw
+
+        gain_rows = keep.tile([P, K_PASS], BF16)
+        nc.vector.memset(gain_rows[:], 0.0)
+        eps = keep.tile([P, 1], F32)
+        nc.vector.memset(eps[:], EPS)
+        ones = keep.tile([P, P], F32)
+        nc.vector.memset(ones[:], 1.0)
+        ident = keep.tile([P, P], F32)
+        make_identity(nc, ident[:])
+        warm = keep.tile([P, 1], F32)
+        nc.scalar.activation(out=warm[:], in_=eps[:], func=ACT.Sqrt)
+
+        nc.sync.dma_start(
+            out=gain_rows[0:PASSES, :], in_=w_rn1.rearrange("(a c) -> a c", c=K_PASS)
+        )
+        x_sb = keep.tile([P, ROW_TILES * D], BF16)
+        for g in range(PASSES):
+            nc.sync.dma_start(
+                out=x_sb[:, g * ROW_TILES * K_PASS : (g + 1) * ROW_TILES * K_PASS].rearrange(
+                    "p (m k) -> p m k", m=ROW_TILES
+                ),
+                in_=x[:, g * K_PASS : (g + 1) * K_PASS].rearrange("(m p) k -> p m k", p=P),
+            )
+        cos_sb = keep.tile([P, ROW_TILES * HALF], BF16)
+        sin_sb = keep.tile([P, ROW_TILES * HALF], BF16)
+        for c in range(RAW_BUFS):
+            load_chunk(c)
+            if c == TABLES_AFTER:
+                for table, table_sb in ((cos, cos_sb), (sin, sin_sb)):
+                    nc.sync.dma_start(
+                        out=table_sb[:].rearrange("p (m j) -> p m j", m=ROW_TILES),
+                        in_=table.rearrange("(m p) j -> p m j", p=P),
+                    )
+
+        gain_t = acc_psum.tile([P, BANK], F32, tag="acc")
+        for u in range(2):
+            nc.tensor.transpose(
+                out=gain_t[:, u * P : (u + 1) * P],
+                in_=gain_rows[:].bitcast(F32)[:, u:PASS_WORDS:2],
+                identity=ident[:],
+            )
+        gain4 = keep.tile([P, 2 * PASSES], F32)
+        nc.vector.tensor_copy(
+            out=gain4[:].rearrange("p (g u) -> p g u", u=2),
+            in_=gain_t[:, 0 : 2 * P].rearrange("p (u g) -> p g u", u=2)[:, 0:PASSES, :],
+        )
+        gain4_bf = gain4[:].bitcast(BF16)
+
+        sumsq = keep.tile([P, ROW_TILES], F32)
+        for m in range(ROW_TILES):
+            squares = keep.tile([P, D], BF16, name="squares%d" % m)
+            nc.scalar.activation(
+                out=squares[:].rearrange("p (g k) -> p g k", g=PASSES),
+                in_=x_sb[:].rearrange("p (g m k) -> p m g k", g=PASSES, m=ROW_TILES)[:, m],
+                func=ACT.Square,
+                accum_out=sumsq[:, m : m + 1],
+            )
+
+        x_words = x_sb[:].bitcast(F32)
+        xg = keep.tile([P, PASSES * S * 4], F32)
+        for g in range(PASSES):
+            x_t = acc_psum.tile([P, BANK], F32, tag="acc")
+            for u in range(2):
+                for m in range(ROW_TILES):
+                    first = (g * ROW_TILES + m) * PASS_WORDS
+                    nc.tensor.transpose(
+                        out=x_t[:, u * S + m * P : u * S + (m + 1) * P],
+                        in_=x_words[:, first + u : first + PASS_WORDS : 2],
+                        identity=ident[:],
+                    )
+            nc.vector.tensor_tensor(
+                out=xg[:, g * S * 4 : (g + 1) * S * 4].rearrange("p (s u e) -> p s u e", u=2, e=2),
+                in0=x_t[:].bitcast(BF16).rearrange("p (u s e) -> p s u e", u=2, e=2),
+                in1=gain4_bf[:, 4 * g : 4 * g + 4]
+                .rearrange("p (o u e) -> p o u e", o=1, u=2)
+                .to_broadcast([P, S, 2, 2]),
+                op=ALU.mult,
+            )
+
+        std = keep.tile([P, ROW_TILES], F32)
+        nc.scalar.activation(out=std[:], in_=sumsq[:], func=ACT.Sqrt, bias=eps[:], scale=1.0 / D)
+        rstd = keep.tile([P, ROW_TILES], F32)
+        nc.vector.reciprocal(out=rstd[:], in_=std[:])
+        rstd_rep = keep.tile([P, S], F32)
+        for m in range(ROW_TILES):
+            nc.vector.tensor_scalar_mul(
+                out=rstd_rep[:, m * P : (m + 1) * P], in0=ones[:], scalar1=rstd[:, m : m + 1]
+            )
+
+        h_codes_of = {}
+        h_scales_of = {}
+
+        def finish_norm(m):
+            rstd_t = acc_psum.tile([P, BANK], F32, tag="acc")
+            nc.tensor.transpose(
+                out=rstd_t[:, 0:P], in_=rstd_rep[:, m * P : (m + 1) * P], identity=ident[:]
+            )
+            h_grouped = keep.tile([P, PASSES * P * 4], BF16, align_bytes=64, name="h_grouped%d" % m)
+            nc.vector.tensor_tensor(
+                out=h_grouped[:].rearrange("p (g s t) -> p g s t", g=PASSES, t=4),
+                in0=xg[:].rearrange("p (g s t) -> p g s t", g=PASSES, t=4)[:, :, m * P : (m + 1) * P, :],
+                in1=rstd_t[:, 0:P]
+                .rearrange("p (o s i) -> p o s i", o=1, i=1)
+                .to_broadcast([P, PASSES, P, 4]),
+                op=ALU.mult,
+            )
+            h_codes = keep.tile([P, PASSES * P], U32, align_bytes=64, name="h_codes%d" % m)
+            h_scales = keep.tile([P, PASSES * P], U8, align_bytes=64, name="h_scales%d" % m)
+            nc.vector.quantize_mx(out=h_codes[:].bitcast(FP8X4), scales=h_scales[:], in_=h_grouped[:])
+            h_codes_of[m] = h_codes
+            h_scales_of[m] = h_scales
+
+        def transpose_chunk(c):
+            raw_words = raw_of[c][:].bitcast(F32)
+            grouped = grouped_pool.tile([P, PASSES * CHUNK * 4], BF16, align_bytes=64)
+            grouped_words = grouped[:].bitcast(F32).rearrange("p (g n u) -> p g n u", g=PASSES, u=2)
+            for g in range(PASSES):
+                flipped = flip_psum.tile([P, BANK], F32)
+                for u in range(2):
+                    for t in range(CHUNK_TILES):
+                        first = t * ROW_WORDS + g * PASS_WORDS
+                        nc.tensor.transpose(
+                            out=flipped[:, u * CHUNK + t * P : u * CHUNK + (t + 1) * P],
+                            in_=raw_words[:, first + u : first + PASS_WORDS : 2],
+                            identity=ident[:],
+                        )
+                nc.scalar.copy(
+                    out=grouped_words[:, g], in_=flipped[:].rearrange("p (u n) -> p n u", u=2)
+                )
+            grouped_of[c] = grouped
+
+        def quantise_chunk(c):
+            i, part = divmod(c, UNIT_CHUNKS)
+            if part == 0:
+                codes = mx_pool.tile([P, PASSES * UNIT], U32, align_bytes=64)
+                scales = mx_pool.tile([P, PASSES * UNIT], U8, align_bytes=64)
+                codes_of[i] = codes
+                scales_of[i] = scales
+            for g in range(PASSES):
+                cols = slice(g * UNIT + part * CHUNK, g * UNIT + (part + 1) * CHUNK)
+                nc.vector.quantize_mx(
+                    out=codes_of[i][:, cols].bitcast(FP8X4),
+                    scales=scales_of[i][:, cols],
+                    in_=grouped_of[c][:, g * CHUNK * 4 : (g + 1) * CHUNK * 4],
+                )
+
+        def multiply(n):
+            i, m = divmod(n, ROW_TILES)
+            acc = acc_psum.tile([P, BANK], F32, tag="acc")
+            for g in range(PASSES):
+                rows = slice(g * P, (g + 1) * P)
+                cols = slice(g * UNIT, (g + 1) * UNIT)
+                nc.tensor.matmul_mx(
+                    out=acc[:],
+                    lhsT=h_codes_of[m][:, rows].bitcast(FP8X4),
+                    lhsT_scale=h_scales_of[m][:, rows],
+                    rhs=codes_of[i][:, cols].bitcast(FP8X4),
+                    rhs_scale=scales_of[i][:, cols],
+                    start=(g == 0),
+                    stop=(g == PASSES - 1),
+                )
+            acc_of[n] = acc
+
+        def empty_bank(n):
+            i, m = divmod(n, ROW_TILES)
+            out, col, kind = units[i][1], units[i][2], units[i][3]
+            acc = acc_of[n]
+            if kind == PLAIN:
+                v_sb = plain_pool.tile([P, UNIT], F32)
+                nc.scalar.copy(out=v_sb[:], in_=acc[:])
+                nc.sync.dma_start(out=out[m * P : (m + 1) * P, col : col + UNIT], in_=v_sb[:])
+            else:
+                pool = first_pool if kind == FIRST else second_pool
+                table_cols = slice(m * HALF + col % HALF, m * HALF + col % HALF + UNIT)
+                by_cos = pool.tile([P, UNIT], F32)
+                by_sin = pool.tile([P, UNIT], F32)
+                nc.vector.tensor_tensor(out=by_cos[:], in0=acc[:], in1=cos_sb[:, table_cols], op=ALU.mult)
+                nc.vector.tensor_tensor(out=by_sin[:], in0=acc[:], in1=sin_sb[:, table_cols], op=ALU.mult)
+                rotated[n] = (by_cos, by_sin)
+
+        def rotary_sums(n):
+            i, m = divmod(n, ROW_TILES)
+            out, col = units[i - 1][1], units[i - 1][2]
+            rows = slice(m * P, (m + 1) * P)
+            y1_cos, y1_sin = rotated[n - ROW_TILES]
+            y2_cos, y2_sin = rotated[n]
+            nc.vector.tensor_tensor(out=y1_cos[:], in0=y1_cos[:], in1=y2_sin[:], op=ALU.subtract)
+            nc.vector.tensor_tensor(out=y1_sin[:], in0=y1_sin[:], in1=y2_cos[:], op=ALU.add)
+            nc.sync.dma_start(out=out[rows, col : col + UNIT], in_=y1_cos[:])
+            nc.sync.dma_start(out=out[rows, HALF + col : HALF + col + UNIT], in_=y1_sin[:])
+
+        multiplied = 0
+        for c in range(CHUNKS + PASS_LAG + 1):
+            if 1 <= c and c + RAW_BUFS - 1 < CHUNKS:
+                load_chunk(c + RAW_BUFS - 1)
+            if c < CHUNKS:
+                transpose_chunk(c)
+            if 1 <= c <= CHUNKS:
+                quantise_chunk(c - 1)
+            if c % UNIT_CHUNKS == 0 and c // UNIT_CHUNKS < ROW_TILES:
+                finish_norm(c // UNIT_CHUNKS)
+            due = c - PASS_LAG + 1 + (1 if c >= CHUNKS - LAST_ROUNDS else 0)
+            for n in range(multiplied, min(due, PRODUCTS)):
+                multiply(n)
+                multiplied = n + 1
+            emptied = c - PASS_LAG - 1
+            if 0 <= emptied < PRODUCTS:
+                empty_bank(emptied)
+            summed = emptied - SUM_LAG
+            if 0 <= summed < PRODUCTS and units[summed // ROW_TILES][3] == SECOND:
+                rotary_sums(summed)

@@ -39,6 +39,8 @@ PLAIN = 2
 
 RAW_BUFS = 8
 TABLES_AFTER = 4
+SORTED = 2
+FIRST_SORTED = 3
 PASS_LAG = 3
 LAST_ROUNDS = 2
 SUM_LAG = 2
@@ -57,12 +59,13 @@ def tile_llamablock_pa_kernel(tc, x, w_rn1, wq, wk, wv, cos, sin, out_0, out_1, 
 
     units = (
         rotary_pair(wq, out_0, 0) + plain(0) + rotary_pair(wq, out_0, UNIT) + plain(1)
-        + rotary_pair(wk, out_1, 0) + rotary_pair(wk, out_1, UNIT) + plain(2) + plain(3)
+        + rotary_pair(wk, out_1, 0) + plain(2) + rotary_pair(wk, out_1, UNIT) + plain(3)
     )
 
     with ExitStack() as ctx:
         keep = ctx.enter_context(tc.tile_pool(name="keep", bufs=1))
         raw_pool = ctx.enter_context(tc.tile_pool(name="raw", bufs=RAW_BUFS))
+        sorted_pool = ctx.enter_context(tc.tile_pool(name="sorted", bufs=3))
         grouped_pool = ctx.enter_context(tc.tile_pool(name="grouped", bufs=4))
         mx_pool = ctx.enter_context(tc.tile_pool(name="mx", bufs=3))
         first_pool = ctx.enter_context(tc.tile_pool(name="first", bufs=4))
@@ -73,6 +76,7 @@ def tile_llamablock_pa_kernel(tc, x, w_rn1, wq, wk, wv, cos, sin, out_0, out_1, 
         ctx.enter_context(tc.manual_schedule())
 
         raw_of = {}
+        sorted_of = {}
         grouped_of = {}
         codes_of = {}
         scales_of = {}
@@ -84,34 +88,34 @@ def tile_llamablock_pa_kernel(tc, x, w_rn1, wq, wk, wv, cos, sin, out_0, out_1, 
             w_dram = units[i][0]
             row = units[i][2] + part * CHUNK
             raw = raw_pool.tile([P, CHUNK_TILES * D], BF16)
-            nc.sync.dma_start(
-                out=raw[:].rearrange("p (t k) -> p t k", t=CHUNK_TILES),
-                in_=w_dram[row : row + CHUNK, :].rearrange("(t p) k -> p t k", p=P),
-            )
+            if c == 0:
+                for t in range(CHUNK_TILES):
+                    nc.sync.dma_start(
+                        out=raw[:, t * D : (t + 1) * D], in_=w_dram[row + t * P : row + (t + 1) * P, :]
+                    )
+            else:
+                nc.sync.dma_start(
+                    out=raw[:].rearrange("p (t k) -> p t k", t=CHUNK_TILES),
+                    in_=w_dram[row : row + CHUNK, :].rearrange("(t p) k -> p t k", p=P),
+                )
             raw_of[c] = raw
 
-        gain_rows = keep.tile([P, K_PASS], BF16)
-        nc.vector.memset(gain_rows[:], 0.0)
         eps = keep.tile([P, 1], F32)
         nc.vector.memset(eps[:], EPS)
-        ones = keep.tile([P, P], F32)
+        ones = keep.tile([P, P], BF16)
         nc.vector.memset(ones[:], 1.0)
+        gain_row = keep.tile([P, D], BF16)
+        nc.vector.memset(gain_row[:], 0.0)
         ident = keep.tile([P, P], F32)
         make_identity(nc, ident[:])
         warm = keep.tile([P, 1], F32)
         nc.scalar.activation(out=warm[:], in_=eps[:], func=ACT.Sqrt)
 
-        nc.sync.dma_start(
-            out=gain_rows[0:PASSES, :], in_=w_rn1.rearrange("(a c) -> a c", c=K_PASS)
-        )
-        x_sb = keep.tile([P, ROW_TILES * D], BF16)
-        for g in range(PASSES):
-            nc.sync.dma_start(
-                out=x_sb[:, g * ROW_TILES * K_PASS : (g + 1) * ROW_TILES * K_PASS].rearrange(
-                    "p (m k) -> p m k", m=ROW_TILES
-                ),
-                in_=x[:, g * K_PASS : (g + 1) * K_PASS].rearrange("(m p) k -> p m k", p=P),
-            )
+        x_of = {}
+        for m in range(ROW_TILES):
+            x_of[m] = keep.tile([P, D], BF16, name="x%d" % m)
+            nc.sync.dma_start(out=x_of[m][:], in_=x[m * P : (m + 1) * P, :])
+        nc.sync.dma_start(out=gain_row[0:1, :], in_=w_rn1.rearrange("(o k) -> o k", o=1))
         cos_sb = keep.tile([P, ROW_TILES * HALF], BF16)
         sin_sb = keep.tile([P, ROW_TILES * HALF], BF16)
         for c in range(RAW_BUFS):
@@ -123,96 +127,102 @@ def tile_llamablock_pa_kernel(tc, x, w_rn1, wq, wk, wv, cos, sin, out_0, out_1, 
                         in_=table.rearrange("(m p) j -> p m j", p=P),
                     )
 
-        gain_t = acc_psum.tile([P, BANK], F32, tag="acc")
-        for u in range(2):
-            nc.tensor.transpose(
-                out=gain_t[:, u * P : (u + 1) * P],
-                in_=gain_rows[:].bitcast(F32)[:, u:PASS_WORDS:2],
-                identity=ident[:],
+        gain_of = []
+        for g in range(PASSES):
+            gain_bank = acc_psum.tile([P, BANK], F32, tag="acc")
+            nc.tensor.matmul(
+                out=gain_bank[:],
+                lhsT=ones[:],
+                rhs=gain_row[:, g * K_PASS : (g + 1) * K_PASS],
+                start=True,
+                stop=True,
             )
-        gain4 = keep.tile([P, 2 * PASSES], F32)
-        nc.vector.tensor_copy(
-            out=gain4[:].rearrange("p (g u) -> p g u", u=2),
-            in_=gain_t[:, 0 : 2 * P].rearrange("p (u g) -> p g u", u=2)[:, 0:PASSES, :],
-        )
-        gain4_bf = gain4[:].bitcast(BF16)
+            gain_of.append(gain_bank)
 
-        sumsq = keep.tile([P, ROW_TILES], F32)
+        h_rows_of = {}
         for m in range(ROW_TILES):
             squares = keep.tile([P, D], BF16, name="squares%d" % m)
-            nc.scalar.activation(
-                out=squares[:].rearrange("p (g k) -> p g k", g=PASSES),
-                in_=x_sb[:].rearrange("p (g m k) -> p m g k", g=PASSES, m=ROW_TILES)[:, m],
-                func=ACT.Square,
-                accum_out=sumsq[:, m : m + 1],
-            )
+            sumsq = keep.tile([P, 1], F32, name="sumsq%d" % m)
+            nc.scalar.activation(out=squares[:], in_=x_of[m][:], func=ACT.Square, accum_out=sumsq[:])
+            std = keep.tile([P, 1], F32, name="std%d" % m)
+            nc.scalar.activation(out=std[:], in_=sumsq[:], func=ACT.Sqrt, bias=eps[:], scale=1.0 / D)
+            rstd = keep.tile([P, 1], F32, name="rstd%d" % m)
+            nc.vector.reciprocal(out=rstd[:], in_=std[:])
+            h_rows = keep.tile([P, D], BF16, name="h_rows%d" % m)
+            for g in range(PASSES):
+                cols = slice(g * K_PASS, (g + 1) * K_PASS)
+                nc.vector.scalar_tensor_tensor(
+                    out=h_rows[:, cols],
+                    in0=x_of[m][:, cols],
+                    scalar=rstd[:],
+                    in1=gain_of[g][:],
+                    op0=ALU.mult,
+                    op1=ALU.mult,
+                )
+            h_rows_of[m] = h_rows
 
-        x_words = x_sb[:].bitcast(F32)
-        xg = keep.tile([P, PASSES * S * 4], F32)
-        for g in range(PASSES):
-            x_t = acc_psum.tile([P, BANK], F32, tag="acc")
-            for u in range(2):
-                for m in range(ROW_TILES):
-                    first = (g * ROW_TILES + m) * PASS_WORDS
-                    nc.tensor.transpose(
-                        out=x_t[:, u * S + m * P : u * S + (m + 1) * P],
-                        in_=x_words[:, first + u : first + PASS_WORDS : 2],
-                        identity=ident[:],
-                    )
-            nc.vector.tensor_tensor(
-                out=xg[:, g * S * 4 : (g + 1) * S * 4].rearrange("p (s u e) -> p s u e", u=2, e=2),
-                in0=x_t[:].bitcast(BF16).rearrange("p (u s e) -> p s u e", u=2, e=2),
-                in1=gain4_bf[:, 4 * g : 4 * g + 4]
-                .rearrange("p (o u e) -> p o u e", o=1, u=2)
-                .to_broadcast([P, S, 2, 2]),
-                op=ALU.mult,
-            )
-
-        std = keep.tile([P, ROW_TILES], F32)
-        nc.scalar.activation(out=std[:], in_=sumsq[:], func=ACT.Sqrt, bias=eps[:], scale=1.0 / D)
-        rstd = keep.tile([P, ROW_TILES], F32)
-        nc.vector.reciprocal(out=rstd[:], in_=std[:])
-        rstd_rep = keep.tile([P, S], F32)
-        for m in range(ROW_TILES):
-            nc.vector.tensor_scalar_mul(
-                out=rstd_rep[:, m * P : (m + 1) * P], in0=ones[:], scalar1=rstd[:, m : m + 1]
-            )
-
+        h_grouped_of = {}
         h_codes_of = {}
         h_scales_of = {}
 
-        def finish_norm(m):
-            rstd_t = acc_psum.tile([P, BANK], F32, tag="acc")
-            nc.tensor.transpose(
-                out=rstd_t[:, 0:P], in_=rstd_rep[:, m * P : (m + 1) * P], identity=ident[:]
-            )
+        def transpose_h(m):
+            words = h_rows_of[m][:].bitcast(F32)
             h_grouped = keep.tile([P, PASSES * P * 4], BF16, align_bytes=64, name="h_grouped%d" % m)
-            nc.vector.tensor_tensor(
-                out=h_grouped[:].rearrange("p (g s t) -> p g s t", g=PASSES, t=4),
-                in0=xg[:].rearrange("p (g s t) -> p g s t", g=PASSES, t=4)[:, :, m * P : (m + 1) * P, :],
-                in1=rstd_t[:, 0:P]
-                .rearrange("p (o s i) -> p o s i", o=1, i=1)
-                .to_broadcast([P, PASSES, P, 4]),
-                op=ALU.mult,
-            )
+            grouped_words = h_grouped[:].bitcast(F32).rearrange("p (g s u) -> p g s u", g=PASSES, u=2)
+            for half in range(PASSES // 2):
+                flipped = flip_psum.tile([P, BANK], F32)
+                for b in range(4):
+                    first = (half * 2 + b // 2) * PASS_WORDS
+                    nc.tensor.transpose(
+                        out=flipped[:, b * P : (b + 1) * P],
+                        in_=words[:, first + b % 2 : first + PASS_WORDS : 2],
+                        identity=ident[:],
+                    )
+                nc.scalar.copy(
+                    out=grouped_words[:, half * 2 : half * 2 + 2],
+                    in_=flipped[:].rearrange("p (g u s) -> p g s u", g=2, u=2),
+                )
+            h_grouped_of[m] = h_grouped
+
+        def quantise_h(m):
             h_codes = keep.tile([P, PASSES * P], U32, align_bytes=64, name="h_codes%d" % m)
             h_scales = keep.tile([P, PASSES * P], U8, align_bytes=64, name="h_scales%d" % m)
-            nc.vector.quantize_mx(out=h_codes[:].bitcast(FP8X4), scales=h_scales[:], in_=h_grouped[:])
+            nc.vector.quantize_mx(
+                out=h_codes[:].bitcast(FP8X4), scales=h_scales[:], in_=h_grouped_of[m][:]
+            )
             h_codes_of[m] = h_codes
             h_scales_of[m] = h_scales
+
+        def sort_chunk(c):
+            words = SORTED * PASS_WORDS
+            by_parity = sorted_pool.tile([P, CHUNK_TILES * words], F32)
+            nc.vector.tensor_copy(
+                out=by_parity[:].rearrange("p (t u j) -> p t u j", t=CHUNK_TILES, u=2),
+                in_=raw_of[c][:]
+                .bitcast(F32)
+                .rearrange("p (t w) -> p t w", t=CHUNK_TILES)[:, :, 0:words]
+                .rearrange("p t (j u) -> p t u j", u=2),
+            )
+            sorted_of[c] = by_parity
 
         def transpose_chunk(c):
             raw_words = raw_of[c][:].bitcast(F32)
             grouped = grouped_pool.tile([P, PASSES * CHUNK * 4], BF16, align_bytes=64)
             grouped_words = grouped[:].bitcast(F32).rearrange("p (g n u) -> p g n u", g=PASSES, u=2)
-            for g in range(PASSES):
+            sorted_passes = SORTED if c in sorted_of else 0
+            for g in list(range(sorted_passes, PASSES)) + list(range(sorted_passes)):
                 flipped = flip_psum.tile([P, BANK], F32)
                 for u in range(2):
                     for t in range(CHUNK_TILES):
-                        first = t * ROW_WORDS + g * PASS_WORDS
+                        if g < sorted_passes:
+                            first = ((t * 2 + u) * SORTED + g) * P
+                            block = sorted_of[c][:, first : first + P]
+                        else:
+                            first = t * ROW_WORDS + g * PASS_WORDS
+                            block = raw_words[:, first + u : first + PASS_WORDS : 2]
                         nc.tensor.transpose(
                             out=flipped[:, u * CHUNK + t * P : u * CHUNK + (t + 1) * P],
-                            in_=raw_words[:, first + u : first + PASS_WORDS : 2],
+                            in_=block,
                             identity=ident[:],
                         )
                 nc.scalar.copy(
@@ -281,22 +291,33 @@ def tile_llamablock_pa_kernel(tc, x, w_rn1, wq, wk, wv, cos, sin, out_0, out_1, 
             nc.sync.dma_start(out=out[rows, HALF + col : HALF + col + UNIT], in_=y1_sin[:])
 
         multiplied = 0
-        for c in range(CHUNKS + PASS_LAG + 1):
+        emptied = 0
+        summed = 0
+        for c in range(CHUNKS + PASS_LAG):
             if 1 <= c and c + RAW_BUFS - 1 < CHUNKS:
                 load_chunk(c + RAW_BUFS - 1)
+            if FIRST_SORTED <= c + 1 < CHUNKS:
+                sort_chunk(c + 1)
             if c < CHUNKS:
                 transpose_chunk(c)
+            if c < ROW_TILES:
+                transpose_h(c)
+            if 1 <= c <= ROW_TILES:
+                quantise_h(c - 1)
             if 1 <= c <= CHUNKS:
                 quantise_chunk(c - 1)
-            if c % UNIT_CHUNKS == 0 and c // UNIT_CHUNKS < ROW_TILES:
-                finish_norm(c // UNIT_CHUNKS)
-            due = c - PASS_LAG + 1 + (1 if c >= CHUNKS - LAST_ROUNDS else 0)
-            for n in range(multiplied, min(due, PRODUCTS)):
+            sums_due = emptied - SUM_LAG if c < CHUNKS else PRODUCTS
+            empties_due = multiplied
+            products_due = c - PASS_LAG + 1 + (1 if c >= CHUNKS - LAST_ROUNDS else 0)
+            for n in range(multiplied, min(products_due, PRODUCTS)):
                 multiply(n)
                 multiplied = n + 1
-            emptied = c - PASS_LAG - 1
-            if 0 <= emptied < PRODUCTS:
-                empty_bank(emptied)
-            summed = emptied - SUM_LAG
-            if 0 <= summed < PRODUCTS and units[summed // ROW_TILES][3] == SECOND:
-                rotary_sums(summed)
+            for n in range(emptied, empties_due):
+                empty_bank(n)
+                emptied = n + 1
+            for n in range(summed, min(sums_due, emptied)):
+                if units[n // ROW_TILES][3] == SECOND:
+                    rotary_sums(n)
+                summed = n + 1
+        for n in range(emptied, PRODUCTS):
+            empty_bank(n)

@@ -27,7 +27,6 @@ BANK = 512
 
 UNIT = 512
 UNITS = 3 * DA // UNIT
-PRODUCTS = UNITS * ROW_TILES
 CHUNK = 256
 CHUNK_TILES = CHUNK // P
 UNIT_CHUNKS = UNIT // CHUNK
@@ -41,9 +40,7 @@ RAW_BUFS = 8
 TABLES_AFTER = 4
 SORTED = 2
 FIRST_SORTED = 3
-PASS_LAG = 3
-LAST_ROUNDS = 2
-SUM_LAG = 2
+TABLES_NEGATED = 4
 
 FLOPS = 2 * S * D * 3 * DA
 
@@ -58,8 +55,8 @@ def tile_llamablock_pa_kernel(tc, x, w_rn1, wq, wk, wv, cos, sin, out_0, out_1, 
         return [(wv, out_2, block * UNIT, PLAIN)]
 
     units = (
-        rotary_pair(wq, out_0, 0) + plain(0) + rotary_pair(wq, out_0, UNIT) + plain(1)
-        + rotary_pair(wk, out_1, 0) + plain(2) + rotary_pair(wk, out_1, UNIT) + plain(3)
+        rotary_pair(wq, out_0, 0) + rotary_pair(wq, out_0, UNIT) + plain(0)
+        + rotary_pair(wk, out_1, 0) + rotary_pair(wk, out_1, UNIT) + plain(1) + plain(2) + plain(3)
     )
 
     with ExitStack() as ctx:
@@ -67,7 +64,7 @@ def tile_llamablock_pa_kernel(tc, x, w_rn1, wq, wk, wv, cos, sin, out_0, out_1, 
         raw_pool = ctx.enter_context(tc.tile_pool(name="raw", bufs=RAW_BUFS))
         sorted_pool = ctx.enter_context(tc.tile_pool(name="sorted", bufs=3))
         grouped_pool = ctx.enter_context(tc.tile_pool(name="grouped", bufs=4))
-        mx_pool = ctx.enter_context(tc.tile_pool(name="mx", bufs=3))
+        mx_pool = ctx.enter_context(tc.tile_pool(name="mx", bufs=4))
         first_pool = ctx.enter_context(tc.tile_pool(name="first", bufs=4))
         second_pool = ctx.enter_context(tc.tile_pool(name="second", bufs=2))
         plain_pool = ctx.enter_context(tc.tile_pool(name="plain", bufs=3))
@@ -116,15 +113,14 @@ def tile_llamablock_pa_kernel(tc, x, w_rn1, wq, wk, wv, cos, sin, out_0, out_1, 
             x_of[m] = keep.tile([P, D], BF16, name="x%d" % m)
             nc.sync.dma_start(out=x_of[m][:], in_=x[m * P : (m + 1) * P, :])
         nc.sync.dma_start(out=gain_row[0:1, :], in_=w_rn1.rearrange("(o k) -> o k", o=1))
-        cos_sb = keep.tile([P, ROW_TILES * HALF], BF16)
-        sin_sb = keep.tile([P, ROW_TILES * HALF], BF16)
+        tables = keep.tile([P, ROW_TILES * 3 * HALF], BF16)
+        tables_by_kind = tables[:].rearrange("p (m f j) -> p m f j", m=ROW_TILES, f=3)
         for c in range(RAW_BUFS):
             load_chunk(c)
             if c == TABLES_AFTER:
-                for table, table_sb in ((cos, cos_sb), (sin, sin_sb)):
+                for kind, table in ((1, cos), (2, sin)):
                     nc.sync.dma_start(
-                        out=table_sb[:].rearrange("p (m j) -> p m j", m=ROW_TILES),
-                        in_=table.rearrange("(m p) j -> p m j", p=P),
+                        out=tables_by_kind[:, :, kind], in_=table.rearrange("(m p) j -> p m j", p=P)
                     )
 
         gain_of = []
@@ -193,30 +189,38 @@ def tile_llamablock_pa_kernel(tc, x, w_rn1, wq, wk, wv, cos, sin, out_0, out_1, 
             h_codes_of[m] = h_codes
             h_scales_of[m] = h_scales
 
-        def sort_chunk(c):
-            words = SORTED * PASS_WORDS
-            by_parity = sorted_pool.tile([P, CHUNK_TILES * words], F32)
-            nc.vector.tensor_copy(
+        def sort_passes(c, first, count, copy):
+            by_parity = sorted_pool.tile([P, CHUNK_TILES * count * PASS_WORDS], F32, tag="sorted%d" % first)
+            copy(
                 out=by_parity[:].rearrange("p (t u j) -> p t u j", t=CHUNK_TILES, u=2),
                 in_=raw_of[c][:]
                 .bitcast(F32)
-                .rearrange("p (t w) -> p t w", t=CHUNK_TILES)[:, :, 0:words]
+                .rearrange("p (t w) -> p t w", t=CHUNK_TILES)[
+                    :, :, first * PASS_WORDS : (first + count) * PASS_WORDS
+                ]
                 .rearrange("p t (j u) -> p t u j", u=2),
             )
-            sorted_of[c] = by_parity
+            for t in range(CHUNK_TILES):
+                for u in range(2):
+                    for g in range(count):
+                        start = ((t * 2 + u) * count + g) * P
+                        sorted_of[c, first + g, t, u] = by_parity[:, start : start + P]
+
+        def sort_chunk(c):
+            sort_passes(c, 0, SORTED, nc.vector.tensor_copy)
+            if c % 2 == 1:
+                sort_passes(c, SORTED, 1, nc.scalar.copy)
 
         def transpose_chunk(c):
             raw_words = raw_of[c][:].bitcast(F32)
             grouped = grouped_pool.tile([P, PASSES * CHUNK * 4], BF16, align_bytes=64)
             grouped_words = grouped[:].bitcast(F32).rearrange("p (g n u) -> p g n u", g=PASSES, u=2)
-            sorted_passes = SORTED if c in sorted_of else 0
-            for g in list(range(sorted_passes, PASSES)) + list(range(sorted_passes)):
+            for g in sorted(range(PASSES), key=lambda g: (c, g, 0, 0) in sorted_of):
                 flipped = flip_psum.tile([P, BANK], F32)
                 for u in range(2):
                     for t in range(CHUNK_TILES):
-                        if g < sorted_passes:
-                            first = ((t * 2 + u) * SORTED + g) * P
-                            block = sorted_of[c][:, first : first + P]
+                        if (c, g, t, u) in sorted_of:
+                            block = sorted_of[c, g, t, u]
                         else:
                             first = t * ROW_WORDS + g * PASS_WORDS
                             block = raw_words[:, first + u : first + PASS_WORDS : 2]
@@ -231,71 +235,69 @@ def tile_llamablock_pa_kernel(tc, x, w_rn1, wq, wk, wv, cos, sin, out_0, out_1, 
             grouped_of[c] = grouped
 
         def quantise_chunk(c):
+            codes = mx_pool.tile([P, PASSES * CHUNK], U32, align_bytes=64)
+            scales = mx_pool.tile([P, PASSES * CHUNK], U8, align_bytes=64)
+            nc.vector.quantize_mx(out=codes[:].bitcast(FP8X4), scales=scales[:], in_=grouped_of[c][:])
+            codes_of[c] = codes
+            scales_of[c] = scales
+
+        def multiply(c):
             i, part = divmod(c, UNIT_CHUNKS)
-            if part == 0:
-                codes = mx_pool.tile([P, PASSES * UNIT], U32, align_bytes=64)
-                scales = mx_pool.tile([P, PASSES * UNIT], U8, align_bytes=64)
-                codes_of[i] = codes
-                scales_of[i] = scales
-            for g in range(PASSES):
-                cols = slice(g * UNIT + part * CHUNK, g * UNIT + (part + 1) * CHUNK)
-                nc.vector.quantize_mx(
-                    out=codes_of[i][:, cols].bitcast(FP8X4),
-                    scales=scales_of[i][:, cols],
-                    in_=grouped_of[c][:, g * CHUNK * 4 : (g + 1) * CHUNK * 4],
-                )
+            for m in range(ROW_TILES):
+                if part == 0:
+                    acc = acc_psum.tile([P, BANK], F32, tag="acc")
+                    acc_of[i, m] = acc
+                for g in range(PASSES):
+                    rows = slice(g * P, (g + 1) * P)
+                    cols = slice(g * CHUNK, (g + 1) * CHUNK)
+                    nc.tensor.matmul_mx(
+                        out=acc_of[i, m][:, part * CHUNK : (part + 1) * CHUNK],
+                        lhsT=h_codes_of[m][:, rows].bitcast(FP8X4),
+                        lhsT_scale=h_scales_of[m][:, rows],
+                        rhs=codes_of[c][:, cols].bitcast(FP8X4),
+                        rhs_scale=scales_of[c][:, cols],
+                        start=(g == 0),
+                        stop=(g == PASSES - 1),
+                    )
 
-        def multiply(n):
-            i, m = divmod(n, ROW_TILES)
-            acc = acc_psum.tile([P, BANK], F32, tag="acc")
-            for g in range(PASSES):
-                rows = slice(g * P, (g + 1) * P)
-                cols = slice(g * UNIT, (g + 1) * UNIT)
-                nc.tensor.matmul_mx(
-                    out=acc[:],
-                    lhsT=h_codes_of[m][:, rows].bitcast(FP8X4),
-                    lhsT_scale=h_scales_of[m][:, rows],
-                    rhs=codes_of[i][:, cols].bitcast(FP8X4),
-                    rhs_scale=scales_of[i][:, cols],
-                    start=(g == 0),
-                    stop=(g == PASSES - 1),
-                )
-            acc_of[n] = acc
-
-        def empty_bank(n):
-            i, m = divmod(n, ROW_TILES)
+        def empty_bank(i, m):
             out, col, kind = units[i][1], units[i][2], units[i][3]
-            acc = acc_of[n]
+            acc = acc_of[i, m]
             if kind == PLAIN:
                 v_sb = plain_pool.tile([P, UNIT], F32)
                 nc.scalar.copy(out=v_sb[:], in_=acc[:])
                 nc.sync.dma_start(out=out[m * P : (m + 1) * P, col : col + UNIT], in_=v_sb[:])
             else:
                 pool = first_pool if kind == FIRST else second_pool
-                table_cols = slice(m * HALF + col % HALF, m * HALF + col % HALF + UNIT)
-                by_cos = pool.tile([P, UNIT], F32)
-                by_sin = pool.tile([P, UNIT], F32)
-                nc.vector.tensor_tensor(out=by_cos[:], in0=acc[:], in1=cos_sb[:, table_cols], op=ALU.mult)
-                nc.vector.tensor_tensor(out=by_sin[:], in0=acc[:], in1=sin_sb[:, table_cols], op=ALU.mult)
-                rotated[n] = (by_cos, by_sin)
+                first_table = 1 if kind == FIRST else 0
+                col %= HALF
+                turned = pool.tile([P, 2 * UNIT], F32)
+                nc.vector.tensor_tensor(
+                    out=turned[:].rearrange("p (f j) -> p f j", f=2),
+                    in0=acc[:].rearrange("p (f j) -> p f j", f=1).to_broadcast([P, 2, UNIT]),
+                    in1=tables_by_kind[:, m, first_table : first_table + 2, col : col + UNIT],
+                    op=ALU.mult,
+                )
+                rotated[i, m] = turned
 
-        def rotary_sums(n):
-            i, m = divmod(n, ROW_TILES)
+        def rotary_sums(i, m):
             out, col = units[i - 1][1], units[i - 1][2]
-            rows = slice(m * P, (m + 1) * P)
-            y1_cos, y1_sin = rotated[n - ROW_TILES]
-            y2_cos, y2_sin = rotated[n]
-            nc.vector.tensor_tensor(out=y1_cos[:], in0=y1_cos[:], in1=y2_sin[:], op=ALU.subtract)
-            nc.vector.tensor_tensor(out=y1_sin[:], in0=y1_sin[:], in1=y2_cos[:], op=ALU.add)
-            nc.sync.dma_start(out=out[rows, col : col + UNIT], in_=y1_cos[:])
-            nc.sync.dma_start(out=out[rows, HALF + col : HALF + col + UNIT], in_=y1_sin[:])
+            result = rotated[i - 1, m]
+            nc.vector.tensor_tensor(out=result[:], in0=result[:], in1=rotated[i, m][:], op=ALU.add)
+            nc.sync.dma_start(
+                out=out.rearrange("r (f j) -> r f j", f=2)[m * P : (m + 1) * P, :, col : col + UNIT],
+                in_=result[:].rearrange("p (f j) -> p f j", f=2),
+            )
 
-        multiplied = 0
-        emptied = 0
-        summed = 0
-        for c in range(CHUNKS + PASS_LAG):
+        to_empty = []
+        to_add = []
+        for c in range(CHUNKS + 4):
             if 1 <= c and c + RAW_BUFS - 1 < CHUNKS:
                 load_chunk(c + RAW_BUFS - 1)
+            if c == TABLES_NEGATED:
+                nc.vector.tensor_scalar_mul(
+                    out=tables_by_kind[:, :, 0], in0=tables_by_kind[:, :, 2], scalar1=-1.0
+                )
             if FIRST_SORTED <= c + 1 < CHUNKS:
                 sort_chunk(c + 1)
             if c < CHUNKS:
@@ -306,18 +308,16 @@ def tile_llamablock_pa_kernel(tc, x, w_rn1, wq, wk, wv, cos, sin, out_0, out_1, 
                 quantise_h(c - 1)
             if 1 <= c <= CHUNKS:
                 quantise_chunk(c - 1)
-            sums_due = emptied - SUM_LAG if c < CHUNKS else PRODUCTS
-            empties_due = multiplied
-            products_due = c - PASS_LAG + 1 + (1 if c >= CHUNKS - LAST_ROUNDS else 0)
-            for n in range(multiplied, min(products_due, PRODUCTS)):
-                multiply(n)
-                multiplied = n + 1
-            for n in range(emptied, empties_due):
-                empty_bank(n)
-                emptied = n + 1
-            for n in range(summed, min(sums_due, emptied)):
-                if units[n // ROW_TILES][3] == SECOND:
-                    rotary_sums(n)
-                summed = n + 1
-        for n in range(emptied, PRODUCTS):
-            empty_bank(n)
+            if 2 <= c < CHUNKS + 2:
+                multiply(c - 2)
+            added = to_add
+            to_add = []
+            for i, m in to_empty[: 1 if c < CHUNKS - 1 else ROW_TILES]:
+                to_empty = to_empty[1:]
+                empty_bank(i, m)
+                if units[i][3] == SECOND:
+                    to_add.append((i, m))
+            for i, m in added:
+                rotary_sums(i, m)
+            if 2 <= c < CHUNKS + 2 and (c - 2) % UNIT_CHUNKS == UNIT_CHUNKS - 1:
+                to_empty += [((c - 2) // UNIT_CHUNKS, m) for m in range(ROW_TILES)]

@@ -39,7 +39,8 @@ PLAIN = 2
 RAW_BUFS = 8
 TABLES_AFTER = 4
 SORTED = 2
-FIRST_SORTED = 3
+SHARED_FROM = 4
+RUN = 8
 TABLES_NEGATED = 4
 
 FLOPS = 2 * S * D * 3 * DA
@@ -97,22 +98,25 @@ def tile_llamablock_pa_kernel(tc, x, w_rn1, wq, wk, wv, cos, sin, out_0, out_1, 
                 )
             raw_of[c] = raw
 
+        gain_row = keep.tile([P, D], BF16)
+        nc.vector.memset(gain_row[:].bitcast(F32), 0.0)
         eps = keep.tile([P, 1], F32)
         nc.vector.memset(eps[:], EPS)
         ones = keep.tile([P, P], BF16)
         nc.vector.memset(ones[:], 1.0)
-        gain_row = keep.tile([P, D], BF16)
-        nc.vector.memset(gain_row[:], 0.0)
         ident = keep.tile([P, P], F32)
         make_identity(nc, ident[:])
         warm = keep.tile([P, 1], F32)
         nc.scalar.activation(out=warm[:], in_=eps[:], func=ACT.Sqrt)
 
+        halves = [slice(0, D // 2), slice(D // 2, D)]
         x_of = {}
         for m in range(ROW_TILES):
             x_of[m] = keep.tile([P, D], BF16, name="x%d" % m)
-            nc.sync.dma_start(out=x_of[m][:], in_=x[m * P : (m + 1) * P, :])
-        nc.sync.dma_start(out=gain_row[0:1, :], in_=w_rn1.rearrange("(o k) -> o k", o=1))
+            for cols in halves if m == 0 else [slice(0, D)]:
+                nc.sync.dma_start(out=x_of[m][:, cols], in_=x[m * P : (m + 1) * P, cols])
+            if m == 0:
+                nc.sync.dma_start(out=gain_row[0:1, :], in_=w_rn1.rearrange("(o k) -> o k", o=1))
         tables = keep.tile([P, ROW_TILES * 3 * HALF], BF16)
         tables_by_kind = tables[:].rearrange("p (m f j) -> p m f j", m=ROW_TILES, f=3)
         for c in range(RAW_BUFS):
@@ -135,27 +139,84 @@ def tile_llamablock_pa_kernel(tc, x, w_rn1, wq, wk, wv, cos, sin, out_0, out_1, 
             )
             gain_of.append(gain_bank)
 
+        def sort_passes(c, first, count, copy):
+            words = slice(first * PASS_WORDS, (first + count) * PASS_WORDS)
+            by_parity = sorted_pool.tile(
+                [P, CHUNK_TILES * count * PASS_WORDS], F32, tag="sorted%d_%d" % (first, count)
+            )
+            copy(
+                out=by_parity[:].rearrange("p (t u q i) -> p t u q i", t=CHUNK_TILES, u=2, i=RUN),
+                in_=raw_of[c][:]
+                .bitcast(F32)
+                .rearrange("p (t w) -> p t w", t=CHUNK_TILES)[:, :, words]
+                .rearrange("p t (q u i) -> p t u q i", u=2, i=RUN),
+            )
+            for t in range(CHUNK_TILES):
+                for u in range(2):
+                    for g in range(count):
+                        start = ((t * 2 + u) * count + g) * P
+                        sorted_of[c, first + g, t, u] = by_parity[:, start : start + P]
+
+        def sort_chunk(c):
+            if c >= SHARED_FROM and c % 2 == 0:
+                sort_passes(c, 0, 1, nc.vector.tensor_copy)
+                sort_passes(c, 1, 1, nc.scalar.copy)
+            else:
+                sort_passes(c, 0, SORTED, nc.vector.tensor_copy)
+
         h_rows_of = {}
         for m in range(ROW_TILES):
             squares = keep.tile([P, D], BF16, name="squares%d" % m)
             sumsq = keep.tile([P, 1], F32, name="sumsq%d" % m)
-            nc.scalar.activation(out=squares[:], in_=x_of[m][:], func=ACT.Square, accum_out=sumsq[:])
+            by_scalar = halves[0] if m == 0 else slice(0, D)
+            nc.scalar.activation(
+                out=squares[:, by_scalar], in_=x_of[m][:, by_scalar], func=ACT.Square, accum_out=sumsq[:]
+            )
+            offset = eps
+            if m == 0:
+                by_vector = halves[1]
+                rest = keep.tile([P, 1], F32)
+                nc.vector.scalar_tensor_tensor(
+                    out=squares[:, by_vector],
+                    in0=x_of[m][:, by_vector],
+                    scalar=1.0,
+                    in1=x_of[m][:, by_vector],
+                    op0=ALU.mult,
+                    op1=ALU.mult,
+                    accum_out=rest[:],
+                )
+                offset = keep.tile([P, 1], F32)
+                nc.vector.tensor_scalar(
+                    out=offset[:], in0=rest[:], scalar1=1.0 / D, scalar2=EPS, op0=ALU.mult, op1=ALU.add
+                )
             std = keep.tile([P, 1], F32, name="std%d" % m)
-            nc.scalar.activation(out=std[:], in_=sumsq[:], func=ACT.Sqrt, bias=eps[:], scale=1.0 / D)
+            nc.scalar.activation(out=std[:], in_=sumsq[:], func=ACT.Sqrt, bias=offset[:], scale=1.0 / D)
             rstd = keep.tile([P, 1], F32, name="rstd%d" % m)
             nc.vector.reciprocal(out=rstd[:], in_=std[:])
             h_rows = keep.tile([P, D], BF16, name="h_rows%d" % m)
             for g in range(PASSES):
                 cols = slice(g * K_PASS, (g + 1) * K_PASS)
-                nc.vector.scalar_tensor_tensor(
-                    out=h_rows[:, cols],
-                    in0=x_of[m][:, cols],
-                    scalar=rstd[:],
-                    in1=gain_of[g][:],
-                    op0=ALU.mult,
-                    op1=ALU.mult,
-                )
+                def by_run(values):
+                    return values.rearrange("p (q u i) -> p u q i", u=2, i=2 * RUN)
+
+                if g < SORTED:
+                    blocks = [
+                        (
+                            h_rows[:, cols].rearrange("p (u q i) -> p u q i", u=2, i=2 * RUN)[:, u],
+                            by_run(x_of[m][:, cols])[:, u],
+                            by_run(gain_of[g][:])[:, u],
+                        )
+                        for u in range(2)
+                    ]
+                else:
+                    blocks = [(h_rows[:, cols], x_of[m][:, cols], gain_of[g][:])]
+                for out, rows, gain in blocks:
+                    nc.vector.scalar_tensor_tensor(
+                        out=out, in0=rows, scalar=rstd[:], in1=gain, op0=ALU.mult, op1=ALU.mult
+                    )
             h_rows_of[m] = h_rows
+            if m == 0:
+                sort_chunk(0)
 
         h_grouped_of = {}
         h_codes_of = {}
@@ -168,10 +229,12 @@ def tile_llamablock_pa_kernel(tc, x, w_rn1, wq, wk, wv, cos, sin, out_0, out_1, 
             for half in range(PASSES // 2):
                 flipped = flip_psum.tile([P, BANK], F32)
                 for b in range(4):
-                    first = (half * 2 + b // 2) * PASS_WORDS
+                    g = half * 2 + b // 2
+                    u = b % 2
+                    rows = words[:, g * PASS_WORDS : (g + 1) * PASS_WORDS]
                     nc.tensor.transpose(
                         out=flipped[:, b * P : (b + 1) * P],
-                        in_=words[:, first + b % 2 : first + PASS_WORDS : 2],
+                        in_=rows[:, u * P : (u + 1) * P] if g < SORTED else rows[:, u::2],
                         identity=ident[:],
                     )
                 nc.scalar.copy(
@@ -189,37 +252,15 @@ def tile_llamablock_pa_kernel(tc, x, w_rn1, wq, wk, wv, cos, sin, out_0, out_1, 
             h_codes_of[m] = h_codes
             h_scales_of[m] = h_scales
 
-        def sort_passes(c, first, count, copy):
-            by_parity = sorted_pool.tile([P, CHUNK_TILES * count * PASS_WORDS], F32, tag="sorted%d" % first)
-            copy(
-                out=by_parity[:].rearrange("p (t u j) -> p t u j", t=CHUNK_TILES, u=2),
-                in_=raw_of[c][:]
-                .bitcast(F32)
-                .rearrange("p (t w) -> p t w", t=CHUNK_TILES)[
-                    :, :, first * PASS_WORDS : (first + count) * PASS_WORDS
-                ]
-                .rearrange("p t (j u) -> p t u j", u=2),
-            )
-            for t in range(CHUNK_TILES):
-                for u in range(2):
-                    for g in range(count):
-                        start = ((t * 2 + u) * count + g) * P
-                        sorted_of[c, first + g, t, u] = by_parity[:, start : start + P]
-
-        def sort_chunk(c):
-            sort_passes(c, 0, SORTED, nc.vector.tensor_copy)
-            if c % 2 == 1:
-                sort_passes(c, SORTED, 1, nc.scalar.copy)
-
         def transpose_chunk(c):
             raw_words = raw_of[c][:].bitcast(F32)
             grouped = grouped_pool.tile([P, PASSES * CHUNK * 4], BF16, align_bytes=64)
             grouped_words = grouped[:].bitcast(F32).rearrange("p (g n u) -> p g n u", g=PASSES, u=2)
-            for g in sorted(range(PASSES), key=lambda g: (c, g, 0, 0) in sorted_of):
+            for g in list(range(SORTED, PASSES)) + list(range(SORTED)):
                 flipped = flip_psum.tile([P, BANK], F32)
                 for u in range(2):
                     for t in range(CHUNK_TILES):
-                        if (c, g, t, u) in sorted_of:
+                        if g < SORTED:
                             block = sorted_of[c, g, t, u]
                         else:
                             first = t * ROW_WORDS + g * PASS_WORDS
@@ -298,7 +339,7 @@ def tile_llamablock_pa_kernel(tc, x, w_rn1, wq, wk, wv, cos, sin, out_0, out_1, 
                 nc.vector.tensor_scalar_mul(
                     out=tables_by_kind[:, :, 0], in0=tables_by_kind[:, :, 2], scalar1=-1.0
                 )
-            if FIRST_SORTED <= c + 1 < CHUNKS:
+            if c + 1 < CHUNKS:
                 sort_chunk(c + 1)
             if c < CHUNKS:
                 transpose_chunk(c)

@@ -39,6 +39,7 @@ PLAIN = 2
 RAW_BUFS = 8
 TABLES_AFTER = 4
 SORTED = 2
+WARM_CHUNKS = 3
 SHARED_FROM = 4
 RUN = 8
 TABLES_NEGATED = 4
@@ -68,7 +69,7 @@ def tile_llamablock_pa_kernel(tc, x, w_rn1, wq, wk, wv, cos, sin, out_0, out_1, 
         mx_pool = ctx.enter_context(tc.tile_pool(name="mx", bufs=4))
         first_pool = ctx.enter_context(tc.tile_pool(name="first", bufs=4))
         second_pool = ctx.enter_context(tc.tile_pool(name="second", bufs=2))
-        plain_pool = ctx.enter_context(tc.tile_pool(name="plain", bufs=3))
+        plain_pool = ctx.enter_context(tc.tile_pool(name="plain", bufs=6))
         flip_psum = ctx.enter_context(tc.psum_pool(name="flip", bufs=4))
         acc_psum = ctx.enter_context(tc.psum_pool(name="acc", bufs=4))
         ctx.enter_context(tc.manual_schedule())
@@ -158,7 +159,7 @@ def tile_llamablock_pa_kernel(tc, x, w_rn1, wq, wk, wv, cos, sin, out_0, out_1, 
                         sorted_of[c, first + g, t, u] = by_parity[:, start : start + P]
 
         def sort_chunk(c):
-            if c >= SHARED_FROM and c % 2 == 0:
+            if c >= SHARED_FROM and c % 4 != 3:
                 sort_passes(c, 0, 1, nc.vector.tensor_copy)
                 sort_passes(c, 1, 1, nc.scalar.copy)
             else:
@@ -252,12 +253,19 @@ def tile_llamablock_pa_kernel(tc, x, w_rn1, wq, wk, wv, cos, sin, out_0, out_1, 
             h_codes_of[m] = h_codes
             h_scales_of[m] = h_scales
 
+        pass_order = list(range(SORTED, PASSES)) + list(range(SORTED))
+
+        def warm_up(bank):
+            nc.tensor.matmul(out=bank[:], lhsT=ones[:], rhs=gain_row[:, 0:BANK], start=True, stop=True)
+
         def transpose_chunk(c):
             raw_words = raw_of[c][:].bitcast(F32)
             grouped = grouped_pool.tile([P, PASSES * CHUNK * 4], BF16, align_bytes=64)
             grouped_words = grouped[:].bitcast(F32).rearrange("p (g n u) -> p g n u", g=PASSES, u=2)
-            for g in list(range(SORTED, PASSES)) + list(range(SORTED)):
+            for g in pass_order:
                 flipped = flip_psum.tile([P, BANK], F32)
+                if c < WARM_CHUNKS and g % 2 == 0:
+                    warm_up(flipped)
                 for u in range(2):
                     for t in range(CHUNK_TILES):
                         if g < SORTED:
@@ -278,7 +286,15 @@ def tile_llamablock_pa_kernel(tc, x, w_rn1, wq, wk, wv, cos, sin, out_0, out_1, 
         def quantise_chunk(c):
             codes = mx_pool.tile([P, PASSES * CHUNK], U32, align_bytes=64)
             scales = mx_pool.tile([P, PASSES * CHUNK], U8, align_bytes=64)
-            nc.vector.quantize_mx(out=codes[:].bitcast(FP8X4), scales=scales[:], in_=grouped_of[c][:])
+            pieces = pass_order if c == CHUNKS - 1 else [0]
+            step = PASSES // len(pieces)
+            for g in pieces:
+                cols = slice(g * CHUNK, (g + step) * CHUNK)
+                nc.vector.quantize_mx(
+                    out=codes[:, cols].bitcast(FP8X4),
+                    scales=scales[:, cols],
+                    in_=grouped_of[c][:, g * CHUNK * 4 : (g + step) * CHUNK * 4],
+                )
             codes_of[c] = codes
             scales_of[c] = scales
 
@@ -288,7 +304,7 @@ def tile_llamablock_pa_kernel(tc, x, w_rn1, wq, wk, wv, cos, sin, out_0, out_1, 
                 if part == 0:
                     acc = acc_psum.tile([P, BANK], F32, tag="acc")
                     acc_of[i, m] = acc
-                for g in range(PASSES):
+                for g in pass_order:
                     rows = slice(g * P, (g + 1) * P)
                     cols = slice(g * CHUNK, (g + 1) * CHUNK)
                     nc.tensor.matmul_mx(
@@ -297,8 +313,8 @@ def tile_llamablock_pa_kernel(tc, x, w_rn1, wq, wk, wv, cos, sin, out_0, out_1, 
                         lhsT_scale=h_scales_of[m][:, rows],
                         rhs=codes_of[c][:, cols].bitcast(FP8X4),
                         rhs_scale=scales_of[c][:, cols],
-                        start=(g == 0),
-                        stop=(g == PASSES - 1),
+                        start=(g == pass_order[0]),
+                        stop=(g == pass_order[-1]),
                     )
 
         def empty_bank(i, m):
@@ -306,7 +322,8 @@ def tile_llamablock_pa_kernel(tc, x, w_rn1, wq, wk, wv, cos, sin, out_0, out_1, 
             acc = acc_of[i, m]
             if kind == PLAIN:
                 v_sb = plain_pool.tile([P, UNIT], F32)
-                nc.scalar.copy(out=v_sb[:], in_=acc[:])
+                copy = nc.vector.tensor_copy if (i, m) == (UNITS - 1, ROW_TILES - 1) else nc.scalar.copy
+                copy(out=v_sb[:], in_=acc[:])
                 nc.sync.dma_start(out=out[m * P : (m + 1) * P, col : col + UNIT], in_=v_sb[:])
             else:
                 pool = first_pool if kind == FIRST else second_pool
@@ -330,6 +347,7 @@ def tile_llamablock_pa_kernel(tc, x, w_rn1, wq, wk, wv, cos, sin, out_0, out_1, 
                 in_=result[:].rearrange("p (f j) -> p f j", f=2),
             )
 
+        last_pair = max(i for i in range(UNITS) if units[i][3] == SECOND)
         to_empty = []
         to_add = []
         for c in range(CHUNKS + 4):
@@ -359,6 +377,9 @@ def tile_llamablock_pa_kernel(tc, x, w_rn1, wq, wk, wv, cos, sin, out_0, out_1, 
                 if units[i][3] == SECOND:
                     to_add.append((i, m))
             for i, m in added:
-                rotary_sums(i, m)
+                if c < CHUNKS and i == last_pair and m == ROW_TILES - 1:
+                    to_add.append((i, m))
+                else:
+                    rotary_sums(i, m)
             if 2 <= c < CHUNKS + 2 and (c - 2) % UNIT_CHUNKS == UNIT_CHUNKS - 1:
                 to_empty += [((c - 2) // UNIT_CHUNKS, m) for m in range(ROW_TILES)]

@@ -39,7 +39,6 @@ PLAIN = 2
 RAW_BUFS = 8
 TABLES_AFTER = 4
 SORTED = 2
-WARM_CHUNKS = 3
 SHARED_FROM = 4
 RUN = 8
 TABLES_NEGATED = 4
@@ -255,17 +254,12 @@ def tile_llamablock_pa_kernel(tc, x, w_rn1, wq, wk, wv, cos, sin, out_0, out_1, 
 
         pass_order = list(range(SORTED, PASSES)) + list(range(SORTED))
 
-        def warm_up(bank):
-            nc.tensor.matmul(out=bank[:], lhsT=ones[:], rhs=gain_row[:, 0:BANK], start=True, stop=True)
-
         def transpose_chunk(c):
             raw_words = raw_of[c][:].bitcast(F32)
             grouped = grouped_pool.tile([P, PASSES * CHUNK * 4], BF16, align_bytes=64)
             grouped_words = grouped[:].bitcast(F32).rearrange("p (g n u) -> p g n u", g=PASSES, u=2)
             for g in pass_order:
                 flipped = flip_psum.tile([P, BANK], F32)
-                if c < WARM_CHUNKS and g % 2 == 0:
-                    warm_up(flipped)
                 for u in range(2):
                     for t in range(CHUNK_TILES):
                         if g < SORTED:

from contextlib import ExitStack

import concourse.mybir as mybir
from concourse.masks import make_identity

BF16 = mybir.dt.bfloat16
F32 = mybir.dt.float32
U32 = mybir.dt.uint32
U8 = mybir.dt.uint8
FP8X4 = mybir.dt.float8_e4m3fn_x4
ACT = mybir.ActivationFunctionType
ALU = mybir.AluOpType

P = 128
S = 256
D = 2048
DA = 2048
HALF = DA // 2
EPS = 1.1920929e-07

ROW_TILES = S // P
K_PASS = 4 * P
PASSES = D // K_PASS
PASS_WORDS = K_PASS // 2
ROW_WORDS = D // 2
BANK = 512

UNIT = 512
UNITS = 3 * DA // UNIT
CHUNK = 256
CHUNK_TILES = CHUNK // P
UNIT_CHUNKS = UNIT // CHUNK
CHUNKS = UNITS * UNIT_CHUNKS

FIRST = 0
SECOND = 1
PLAIN = 2

RAW_BUFS = 8
TABLES_AFTER = 4
SORTED = 2
SHARED_FROM = 4
RUN = 8
TABLES_NEGATED = 4

FLOPS = 2 * S * D * 3 * DA


def tile_llamablock_pa_kernel(tc, x, w_rn1, wq, wk, wv, cos, sin, out_0, out_1, out_2):
    nc = tc.nc

    def rotary_pair(w, out, col):
        return [(w, out, col, FIRST), (w, out, HALF + col, SECOND)]

    def plain(block):
        return [(wv, out_2, block * UNIT, PLAIN)]

    units = (
        rotary_pair(wq, out_0, 0) + rotary_pair(wq, out_0, UNIT) + plain(0)
        + rotary_pair(wk, out_1, 0) + rotary_pair(wk, out_1, UNIT) + plain(1) + plain(2) + plain(3)
    )

    with ExitStack() as ctx:
        keep = ctx.enter_context(tc.tile_pool(name="keep", bufs=1))
        raw_pool = ctx.enter_context(tc.tile_pool(name="raw", bufs=RAW_BUFS))
        sorted_pool = ctx.enter_context(tc.tile_pool(name="sorted", bufs=3))
        grouped_pool = ctx.enter_context(tc.tile_pool(name="grouped", bufs=4))
        mx_pool = ctx.enter_context(tc.tile_pool(name="mx", bufs=4))
        first_pool = ctx.enter_context(tc.tile_pool(name="first", bufs=4))
        second_pool = ctx.enter_context(tc.tile_pool(name="second", bufs=2))
        plain_pool = ctx.enter_context(tc.tile_pool(name="plain", bufs=6))
        flip_psum = ctx.enter_context(tc.psum_pool(name="flip", bufs=4))
        acc_psum = ctx.enter_context(tc.psum_pool(name="acc", bufs=4))
        ctx.enter_context(tc.manual_schedule())

        raw_of = {}
        sorted_of = {}
        grouped_of = {}
        codes_of = {}
        scales_of = {}
        acc_of = {}
        rotated = {}

        def load_chunk(c):
            i, part = divmod(c, UNIT_CHUNKS)
            w_dram = units[i][0]
            row = units[i][2] + part * CHUNK
            raw = raw_pool.tile([P, CHUNK_TILES * D], BF16)
            if c == 0:
                for t in range(CHUNK_TILES):
                    nc.sync.dma_start(
                        out=raw[:, t * D : (t + 1) * D], in_=w_dram[row + t * P : row + (t + 1) * P, :]
                    )
            else:
                nc.sync.dma_start(
                    out=raw[:].rearrange("p (t k) -> p t k", t=CHUNK_TILES),
                    in_=w_dram[row : row + CHUNK, :].rearrange("(t p) k -> p t k", p=P),
                )
            raw_of[c] = raw

        gain_row = keep.tile([P, D], BF16)
        nc.vector.memset(gain_row[:].bitcast(F32), 0.0)
        eps = keep.tile([P, 1], F32)
        nc.vector.memset(eps[:], EPS)
        ones = keep.tile([P, P], BF16)
        nc.vector.memset(ones[:], 1.0)
        ident = keep.tile([P, P], F32)
        make_identity(nc, ident[:])
        warm = keep.tile([P, 1], F32)
        nc.scalar.activation(out=warm[:], in_=eps[:], func=ACT.Sqrt)

        halves = [slice(0, D // 2), slice(D // 2, D)]
        x_of = {}
        for m in range(ROW_TILES):
            x_of[m] = keep.tile([P, D], BF16, name="x%d" % m)
            for cols in halves if m == 0 else [slice(0, D)]:
                nc.sync.dma_start(out=x_of[m][:, cols], in_=x[m * P : (m + 1) * P, cols])
            if m == 0:
                nc.sync.dma_start(out=gain_row[0:1, :], in_=w_rn1.rearrange("(o k) -> o k", o=1))
        tables = keep.tile([P, ROW_TILES * 3 * HALF], BF16)
        tables_by_kind = tables[:].rearrange("p (m f j) -> p m f j", m=ROW_TILES, f=3)
        for c in range(RAW_BUFS):
            load_chunk(c)
            if c == TABLES_AFTER:
                for kind, table in ((1, cos), (2, sin)):
                    nc.sync.dma_start(
                        out=tables_by_kind[:, :, kind], in_=table.rearrange("(m p) j -> p m j", p=P)
                    )

        gain_of = []
        for g in range(PASSES):
            gain_bank = acc_psum.tile([P, BANK], F32, tag="acc")
            nc.tensor.matmul(
                out=gain_bank[:],
                lhsT=ones[:],
                rhs=gain_row[:, g * K_PASS : (g + 1) * K_PASS],
                start=True,
                stop=True,
            )
            gain_of.append(gain_bank)

        def sort_passes(c, first, count, copy):
            words = slice(first * PASS_WORDS, (first + count) * PASS_WORDS)
            by_parity = sorted_pool.tile(
                [P, CHUNK_TILES * count * PASS_WORDS], F32, tag="sorted%d_%d" % (first, count)
            )
            copy(
                out=by_parity[:].rearrange("p (t u q i) -> p t u q i", t=CHUNK_TILES, u=2, i=RUN),
                in_=raw_of[c][:]
                .bitcast(F32)
                .rearrange("p (t w) -> p t w", t=CHUNK_TILES)[:, :, words]
                .rearrange("p t (q u i) -> p t u q i", u=2, i=RUN),
            )
            for t in range(CHUNK_TILES):
                for u in range(2):
                    for g in range(count):
                        start = ((t * 2 + u) * count + g) * P
                        sorted_of[c, first + g, t, u] = by_parity[:, start : start + P]

        def sort_chunk(c):
            if c >= SHARED_FROM and c % 4 != 3:
                sort_passes(c, 0, 1, nc.vector.tensor_copy)
                sort_passes(c, 1, 1, nc.scalar.copy)
            else:
                sort_passes(c, 0, SORTED, nc.vector.tensor_copy)

        h_rows_of = {}
        for m in range(ROW_TILES):
            squares = keep.tile([P, D], BF16, name="squares%d" % m)
            sumsq = keep.tile([P, 1], F32, name="sumsq%d" % m)
            by_scalar = halves[0] if m == 0 else slice(0, D)
            nc.scalar.activation(
                out=squares[:, by_scalar], in_=x_of[m][:, by_scalar], func=ACT.Square, accum_out=sumsq[:]
            )
            offset = eps
            if m == 0:
                by_vector = halves[1]
                rest = keep.tile([P, 1], F32)
                nc.vector.scalar_tensor_tensor(
                    out=squares[:, by_vector],
                    in0=x_of[m][:, by_vector],
                    scalar=1.0,
                    in1=x_of[m][:, by_vector],
                    op0=ALU.mult,
                    op1=ALU.mult,
                    accum_out=rest[:],
                )
                offset = keep.tile([P, 1], F32)
                nc.vector.tensor_scalar(
                    out=offset[:], in0=rest[:], scalar1=1.0 / D, scalar2=EPS, op0=ALU.mult, op1=ALU.add
                )
            std = keep.tile([P, 1], F32, name="std%d" % m)
            nc.scalar.activation(out=std[:], in_=sumsq[:], func=ACT.Sqrt, bias=offset[:], scale=1.0 / D)
            rstd = keep.tile([P, 1], F32, name="rstd%d" % m)
            nc.vector.reciprocal(out=rstd[:], in_=std[:])
            h_rows = keep.tile([P, D], BF16, name="h_rows%d" % m)
            for g in range(PASSES):
                cols = slice(g * K_PASS, (g + 1) * K_PASS)
                def by_run(values):
                    return values.rearrange("p (q u i) -> p u q i", u=2, i=2 * RUN)

                if g < SORTED:
                    blocks = [
                        (
                            h_rows[:, cols].rearrange("p (u q i) -> p u q i", u=2, i=2 * RUN)[:, u],
                            by_run(x_of[m][:, cols])[:, u],
                            by_run(gain_of[g][:])[:, u],
                        )
                        for u in range(2)
                    ]
                else:
                    blocks = [(h_rows[:, cols], x_of[m][:, cols], gain_of[g][:])]
                for out, rows, gain in blocks:
                    nc.vector.scalar_tensor_tensor(
                        out=out, in0=rows, scalar=rstd[:], in1=gain, op0=ALU.mult, op1=ALU.mult
                    )
            h_rows_of[m] = h_rows
            if m == 0:
                sort_chunk(0)

        h_grouped_of = {}
        h_codes_of = {}
        h_scales_of = {}

        def transpose_h(m):
            words = h_rows_of[m][:].bitcast(F32)
            h_grouped = keep.tile([P, PASSES * P * 4], BF16, align_bytes=64, name="h_grouped%d" % m)
            grouped_words = h_grouped[:].bitcast(F32).rearrange("p (g s u) -> p g s u", g=PASSES, u=2)
            for half in range(PASSES // 2):
                flipped = flip_psum.tile([P, BANK], F32)
                for b in range(4):
                    g = half * 2 + b // 2
                    u = b % 2
                    rows = words[:, g * PASS_WORDS : (g + 1) * PASS_WORDS]
                    nc.tensor.transpose(
                        out=flipped[:, b * P : (b + 1) * P],
                        in_=rows[:, u * P : (u + 1) * P] if g < SORTED else rows[:, u::2],
                        identity=ident[:],
                    )
                nc.scalar.copy(
                    out=grouped_words[:, half * 2 : half * 2 + 2],
                    in_=flipped[:].rearrange("p (g u s) -> p g s u", g=2, u=2),
                )
            h_grouped_of[m] = h_grouped

        def quantise_h(m):
            h_codes = keep.tile([P, PASSES * P], U32, align_bytes=64, name="h_codes%d" % m)
            h_scales = keep.tile([P, PASSES * P], U8, align_bytes=64, name="h_scales%d" % m)
            nc.vector.quantize_mx(
                out=h_codes[:].bitcast(FP8X4), scales=h_scales[:], in_=h_grouped_of[m][:]
            )
            h_codes_of[m] = h_codes
            h_scales_of[m] = h_scales

        pass_order = list(range(SORTED, PASSES)) + list(range(SORTED))

        def transpose_chunk(c):
            raw_words = raw_of[c][:].bitcast(F32)
            grouped = grouped_pool.tile([P, PASSES * CHUNK * 4], BF16, align_bytes=64)
            grouped_words = grouped[:].bitcast(F32).rearrange("p (g n u) -> p g n u", g=PASSES, u=2)
            for g in pass_order:
                flipped = flip_psum.tile([P, BANK], F32)
                for u in range(2):
                    for t in range(CHUNK_TILES):
                        if g < SORTED:
                            block = sorted_of[c, g, t, u]
                        else:
                            first = t * ROW_WORDS + g * PASS_WORDS
                            block = raw_words[:, first + u : first + PASS_WORDS : 2]
                        nc.tensor.transpose(
                            out=flipped[:, u * CHUNK + t * P : u * CHUNK + (t + 1) * P],
                            in_=block,
                            identity=ident[:],
                        )
                nc.scalar.copy(
                    out=grouped_words[:, g], in_=flipped[:].rearrange("p (u n) -> p n u", u=2)
                )
            grouped_of[c] = grouped

        def quantise_chunk(c):
            codes = mx_pool.tile([P, PASSES * CHUNK], U32, align_bytes=64)
            scales = mx_pool.tile([P, PASSES * CHUNK], U8, align_bytes=64)
            pieces = pass_order if c == CHUNKS - 1 else [0]
            step = PASSES // len(pieces)
            for g in pieces:
                cols = slice(g * CHUNK, (g + step) * CHUNK)
                nc.vector.quantize_mx(
                    out=codes[:, cols].bitcast(FP8X4),
                    scales=scales[:, cols],
                    in_=grouped_of[c][:, g * CHUNK * 4 : (g + step) * CHUNK * 4],
                )
            codes_of[c] = codes
            scales_of[c] = scales

        def multiply(c):
            i, part = divmod(c, UNIT_CHUNKS)
            for m in range(ROW_TILES):
                if part == 0:
                    acc = acc_psum.tile([P, BANK], F32, tag="acc")
                    acc_of[i, m] = acc
                for g in pass_order:
                    rows = slice(g * P, (g + 1) * P)
                    cols = slice(g * CHUNK, (g + 1) * CHUNK)
                    nc.tensor.matmul_mx(
                        out=acc_of[i, m][:, part * CHUNK : (part + 1) * CHUNK],
                        lhsT=h_codes_of[m][:, rows].bitcast(FP8X4),
                        lhsT_scale=h_scales_of[m][:, rows],
                        rhs=codes_of[c][:, cols].bitcast(FP8X4),
                        rhs_scale=scales_of[c][:, cols],
                        start=(g == pass_order[0]),
                        stop=(g == pass_order[-1]),
                    )

        def empty_bank(i, m):
            out, col, kind = units[i][1], units[i][2], units[i][3]
            acc = acc_of[i, m]
            if kind == PLAIN:
                v_sb = plain_pool.tile([P, UNIT], F32)
                copy = nc.vector.tensor_copy if (i, m) == (UNITS - 1, ROW_TILES - 1) else nc.scalar.copy
                copy(out=v_sb[:], in_=acc[:])
                nc.sync.dma_start(out=out[m * P : (m + 1) * P, col : col + UNIT], in_=v_sb[:])
            else:
                pool = first_pool if kind == FIRST else second_pool
                first_table = 1 if kind == FIRST else 0
                col %= HALF
                turned = pool.tile([P, 2 * UNIT], F32)
                nc.vector.tensor_tensor(
                    out=turned[:].rearrange("p (f j) -> p f j", f=2),
                    in0=acc[:].rearrange("p (f j) -> p f j", f=1).to_broadcast([P, 2, UNIT]),
                    in1=tables_by_kind[:, m, first_table : first_table + 2, col : col + UNIT],
                    op=ALU.mult,
                )
                rotated[i, m] = turned

        def rotary_sums(i, m):
            out, col = units[i - 1][1], units[i - 1][2]
            result = rotated[i - 1, m]
            nc.vector.tensor_tensor(out=result[:], in0=result[:], in1=rotated[i, m][:], op=ALU.add)
            nc.sync.dma_start(
                out=out.rearrange("r (f j) -> r f j", f=2)[m * P : (m + 1) * P, :, col : col + UNIT],
                in_=result[:].rearrange("p (f j) -> p f j", f=2),
            )

        last_pair = max(i for i in range(UNITS) if units[i][3] == SECOND)
        to_empty = []
        to_add = []
        for c in range(CHUNKS + 4):
            if 1 <= c and c + RAW_BUFS - 1 < CHUNKS:
                load_chunk(c + RAW_BUFS - 1)
            if c == TABLES_NEGATED:
                nc.vector.tensor_scalar_mul(
                    out=tables_by_kind[:, :, 0], in0=tables_by_kind[:, :, 2], scalar1=-1.0
                )
            if c + 1 < CHUNKS:
                sort_chunk(c + 1)
            if c < CHUNKS:
                transpose_chunk(c)
            if c < ROW_TILES:
                transpose_h(c)
            if 1 <= c <= ROW_TILES:
                quantise_h(c - 1)
            if 1 <= c <= CHUNKS:
                quantise_chunk(c - 1)
            if 2 <= c < CHUNKS + 2:
                multiply(c - 2)
            added = to_add
            to_add = []
            for i, m in to_empty[: 1 if c < CHUNKS - 1 else ROW_TILES]:
                to_empty = to_empty[1:]
                empty_bank(i, m)
                if units[i][3] == SECOND:
                    to_add.append((i, m))
            for i, m in added:
                if c < CHUNKS and i == last_pair and m == ROW_TILES - 1:
                    to_add.append((i, m))
                else:
                    rotary_sums(i, m)
            if 2 <= c < CHUNKS + 2 and (c - 2) % UNIT_CHUNKS == UNIT_CHUNKS - 1:
                to_empty += [((c - 2) // UNIT_CHUNKS, m) for m in range(ROW_TILES)]
